import numpy as np
import ml_dtypes


def mxq(x, axis, fmt="e4m3"):
    dtype, down = {"e4m3": (ml_dtypes.float8_e4m3fn, 7), "e5m2": (ml_dtypes.float8_e5m2, 14)}[fmt]
    v = np.moveaxis(np.asarray(x, np.float32).astype(ml_dtypes.bfloat16).astype(np.float64), axis, -1)
    blocks = v.reshape(v.shape[:-1] + (-1, 32))
    amax = np.abs(blocks).max(-1, keepdims=True)
    byte = np.maximum(np.where(amax > 0, np.frexp(amax)[1] - 1 + 127, 0) - down, 1)
    scale = np.exp2(byte - 127.0)
    codes = (blocks / scale).astype(np.float32).astype(dtype).astype(np.float64)
    return np.moveaxis((codes * scale).reshape(v.shape), -1, axis)


WIDE = False


def mx_kscale(k):
    if not WIDE:
        return np.ones(k)
    levels = np.array([10, -10, 5, -5, 0])
    if k % 512:
        return np.exp2(np.random.permutation(np.resize(levels, k // 32))).repeat(32)
    a = np.empty((k // 512, 16))
    for p in range(k // 512):
        a[p, :8] = np.random.permutation(np.resize(levels, 8))
        for g in range(8):
            far = levels[np.abs(levels - a[p, g]) >= 10]
            a[p, g + 8] = far[np.random.randint(len(far))]
    return np.exp2(a.ravel()).repeat(32)


BF16 = ml_dtypes.bfloat16


def bf(x):
    return np.asarray(x, np.float32).astype(BF16)


def f64(x):
    return np.asarray(x).astype(np.float64)


B, T, E, H, DK, C = 1, 1024, 1024, 4, 256, 512
DV = 2 * DK
F = H * DV
EPS = 1e-5


def draw0():
    s, t = mx_kscale(E), mx_kscale(F)
    o = np.random.standard_normal((B, T, H, DV)) * 5.0 * np.exp(0.5 * np.random.standard_normal((B, T, H, 1)))
    return {"o_ret": bf(o),
            "x": bf(np.random.standard_normal((B, T, E)) * s),
            "Wg": bf(np.random.standard_normal((E, F)) / np.sqrt(E) / s[:, None] * t),
            "gn_weight": bf(1.0 + 0.1 * np.random.standard_normal(DV)),
            "Wo": bf(np.random.standard_normal((F, E)) / np.sqrt(F) / t[:, None])}


def core(o_ret, x, Wg, gn_weight, Wo):
    o = f64(o_ret)
    rms = np.sqrt(np.mean(o * o, axis=-1, keepdims=True) + EPS)
    o = o / rms * f64(gn_weight)
    g = mxq(f64(x), 2, "e4m3") @ mxq(f64(Wg), 0, "e4m3")
    h = o.reshape(B, T, F) * g
    return mxq(h, 2, "e4m3") @ mxq(f64(Wo), 0, "e4m3")


def e4m3fn_bytes(y):
    return np.clip(np.asarray(y, np.float64), -448.0, 448.0).astype(np.float32).astype(ml_dtypes.float8_e4m3fn).view(np.uint8)


def e4m3fn_values(b):
    return np.asarray(b, np.uint8).view(ml_dtypes.float8_e4m3fn).astype(np.float64)


def setup_inputs():
    d = draw0()
    x0 = np.asarray(d['Wo']).astype(np.float64)
    s = (np.max(np.abs(x0), axis=(1,), keepdims=True) / 448.0).astype(np.float32)
    out = {}
    for k, v in d.items():
        if k == 'Wo':
            out['Wo_bytes'] = e4m3fn_bytes(x0 / s.astype(np.float64))
            out['Wo_scale'] = s
        else:
            out[k] = v
    return out


def reference(o_ret, x, Wg, gn_weight, Wo_bytes, Wo_scale):
    return core(o_ret, x, Wg, gn_weight, e4m3fn_values(Wo_bytes) * Wo_scale.astype(np.float64))

from contextlib import ExitStack

import concourse.mybir as mybir
from concourse.masks import make_identity

TOKENS, E, HEADS, DV = 1024, 1024, 4, 512
F = HEADS * DV
N_OUT = 1024
EPS = 1e-5

P = 128
PACK = 4
K_PASS = P * PACK
HALF = 512
N_HALVES = TOKENS // HALF
TILES = TOKENS // P
X_PASSES = E // K_PASS
H_PASSES = F // K_PASS

FLOPS = 2 * TOKENS * E * F + 2 * TOKENS * F * N_OUT

F32 = mybir.dt.float32
BF16 = mybir.dt.bfloat16
U32 = mybir.dt.uint32
U8 = mybir.dt.uint8
FP8 = mybir.dt.float8_e4m3fn
FP8X4 = mybir.dt.float8_e4m3fn_x4
MULT = mybir.AluOpType.mult
ADD = mybir.AluOpType.add
POW = mybir.AluOpType.pow
ACT = mybir.ActivationFunctionType

SW_A = ((),(),(),())
SW_B = (0,1,2,3)
GATES_EARLY = 2
GATE_STEP = 0
WIDEN_B = {0:(0,1),1:(2,3)}
B_INT = {1:(0,1),2:(2,3)}
B_Q = {1:(0,1),2:(2,3)}
B_G = ()
OUTV = (0,)*8
MAXB = (2,)*8


def tile_multiscaleretention_pc_kernel(tc, o_ret, x, Wg, gn_weight, Wo_bytes, Wo_scale, out):
    nc = tc.nc
    x_rows = x[0].rearrange("(q a p) k -> q p a k", a=2, p=P)
    o_rows = o_ret[0].rearrange("(i p) h d -> i p (h d)", p=P)
    wg_rows = Wg.rearrange("(g p j) f -> g p j f", p=P, j=PACK)
    wo_rows = Wo_bytes.rearrange("(g p j) n -> g p j n", p=P, j=PACK)
    out_rows = out[0].rearrange("(i p) n -> i p n", p=P)

    with ExitStack() as ctx:
        const = ctx.enter_context(tc.tile_pool(name="const", bufs=1))
        keep = ctx.enter_context(tc.tile_pool(name="keep", bufs=1))
        inp = ctx.enter_context(tc.tile_pool(name="inp", bufs=8))
        bytes_in = ctx.enter_context(tc.tile_pool(name="bytes_in", bufs=4))
        grp = ctx.enter_context(tc.tile_pool(name="grp", bufs=7))
        small = ctx.enter_context(tc.tile_pool(name="small", bufs=3))
        norm = ctx.enter_context(tc.tile_pool(name="norm", bufs=8))
        hq = ctx.enter_context(tc.tile_pool(name="hq", bufs=6))
        res = ctx.enter_context(tc.tile_pool(name="res", bufs=3))
        ps_turn = ctx.enter_context(tc.psum_pool(name="ps_turn", bufs=4))
        ps_gate = ctx.enter_context(tc.psum_pool(name="ps_gate", bufs=2))
        ps_out = ctx.enter_context(tc.psum_pool(name="ps_out", bufs=2))
        ctx.enter_context(tc.manual_schedule())

        x_codes = keep.tile([P, X_PASSES, TOKENS], U32, align_bytes=64, name="x_codes")
        x_scales = keep.tile([P, X_PASSES, TOKENS], U8, align_bytes=64, name="x_scales")
        wg_codes = keep.tile([P, X_PASSES, F], U32, align_bytes=64, name="wg_codes")
        wg_scales = keep.tile([P, X_PASSES, F], U8, align_bytes=64, name="wg_scales")
        wo_codes = keep.tile([P, H_PASSES, N_OUT], U32, align_bytes=64, name="wo_codes")
        wo_scales = keep.tile([P, H_PASSES, N_OUT], U8, align_bytes=64, name="wo_scales")
        gated = [[keep.tile([P, PACK, HALF], F32, name=f"gated_{h}_{s}") for s in range(N_HALVES)] for h in range(HEADS)]

        ident = const.tile([P, P], F32, name="ident")
        gn_raw = const.tile([P, PACK], BF16, name="gn_raw")
        gn = const.tile([P, PACK], F32, name="gn")
        wo_k_scale = const.tile([P, H_PASSES, PACK], F32, name="wo_k_scale")
        neg_half = const.tile([P, HEADS], F32, name="neg_half")
        warm = const.tile([P, 1], F32, name="warm")

        def load_x(q):
            t = inp.tile([P, 2, E], BF16, tag="inp", name="x_raw", align_bytes=64)
            nc.sync.dma_start(out=t[:], in_=x_rows[q])
            return t

        def load_wg(h, g):
            t = inp.tile([P, PACK, DV], BF16, tag="inp", name="wg_raw", align_bytes=64)
            nc.sync.dma_start(out=t[:], in_=wg_rows[g, :, :, h * DV : (h + 1) * DV])
            return t

        def load_o(i):
            t = inp.tile([P, F], BF16, tag="inp", name="o_raw", align_bytes=64)
            nc.sync.dma_start(out=t[:], in_=o_rows[i])
            return t

        def load_wo(g):
            t = bytes_in.tile([P, PACK, N_OUT], U8, tag="wo_raw", name="wo_raw", align_bytes=64)
            nc.sync.dma_start(out=t[:], in_=wo_rows[g])
            return t

        def group_tile(name):
            return grp.tile([P, K_PASS * PACK], BF16, tag="grp", name=name, align_bytes=64)

        def quantize(grouped, codes, scales):
            nc.vector.quantize_mx(out=codes.bitcast(FP8X4), scales=scales, in_=grouped[:])

        def turn_x(raw, q, grouped):
            words = raw[:].rearrange("p a k -> p (a k)").bitcast(F32)
            for g in range(X_PASSES):
                bank = ps_turn.tile([P, 2, 2, P], F32, tag="turn", name="x_turned")
                for a in range(2):
                    for u in range(2):
                        lo = a * (E // 2) + g * (K_PASS // 2)
                        nc.tensor.transpose(bank[:, a, u, :], words[:, lo + u : lo + K_PASS // 2 : 2], ident[:])
                pairs = grouped[g][:].bitcast(F32).rearrange("p (s a r u) -> p s a r u", s=2, a=2, u=2)
                nc.scalar.copy(out=pairs[:, q % 2], in_=bank[:].rearrange("p a u r -> p a r u"))

        def quantize_x(grouped, s):
            for g in range(X_PASSES):
                cols = slice(s * HALF, (s + 1) * HALF)
                quantize(grouped[g], x_codes[:, g, cols], x_scales[:, g, cols])

        def interleave_wg(raw):
            grouped = group_tile("wg_grouped")
            nc.vector.tensor_copy(
                out=grouped[:].rearrange("p (t m j) -> p t m j", t=PACK, j=PACK),
                in_=raw[:].rearrange("p j (m t) -> p t m j", t=PACK),
            )
            return grouped

        def quantize_wg(grouped, h, g):
            cols = slice(h * DV, (h + 1) * DV)
            quantize(grouped, wg_codes[:, g, cols], wg_scales[:, g, cols])

        def prepare_wg(h, raws):
            grouped = [interleave_wg(raws[g]) for g in range(X_PASSES)]
            for g in range(X_PASSES):
                quantize_wg(grouped[g], h, g)

        def gate(h, s):
            toks = slice(s * HALF, (s + 1) * HALF)
            for t in range(PACK):
                bank = ps_gate.tile([P, HALF], F32, tag="gate", name="gate_bank")
                cols = slice(h * DV + t * P, h * DV + (t + 1) * P)
                for g in range(X_PASSES):
                    nc.tensor.matmul_mx(
                        out=bank[:],
                        lhsT=wg_codes[:, g, cols].bitcast(FP8X4),
                        lhsT_scale=wg_scales[:, g, cols],
                        rhs=x_codes[:, g, toks].bitcast(FP8X4),
                        rhs_scale=x_scales[:, g, toks],
                        start=(g == 0),
                        stop=(g == X_PASSES - 1),
                    )
                nc.scalar.activation(out=gated[h][s][:, t, :], in_=bank[:], func=ACT.Copy, scale=gn[:, t : t + 1])

        def widen(raw, g, n, on_scalar):
            wide = group_tile("wo_wide")
            cols = slice(n * HALF, (n + 1) * HALF)
            for t in range(PACK):
                src = raw[:, t, cols].bitcast(FP8)
                dst = wide[:, t * HALF : (t + 1) * HALF]
                scale = wo_k_scale[:, g, t : t + 1]
                if t in on_scalar:
                    nc.scalar.activation(out=dst, in_=src, func=ACT.Copy, scale=scale)
                else:
                    nc.vector.tensor_scalar(out=dst, in0=src, scalar1=scale, scalar2=None, op0=MULT)
            return wide

        def interleave_wo(wide, on_gpsimd=False):
            grouped = group_tile("wo_grouped")
            dst = grouped[:].rearrange("p (c j) -> p c j", j=PACK)
            src = wide[:].rearrange("p (j c) -> p c j", j=PACK)
            if on_gpsimd:
                nc.gpsimd.tensor_scalar(out=dst, in0=src, scalar1=1.0, scalar2=1.0, op0=MULT, op1=MULT)
            else:
                nc.vector.tensor_copy(out=dst, in_=src)
            return grouped

        def quantize_wo(grouped, g, n):
            cols = slice(n * HALF, (n + 1) * HALF)
            quantize(grouped, wo_codes[:, g, cols], wo_scales[:, g, cols])

        def stats(o_sb):
            ss = small.tile([P, HEADS], F32, tag="ss", name="ss")
            for h in range(HEADS):
                sq = small.tile([P, DV], BF16, tag="sq", name="sq")
                nc.scalar.activation(out=sq[:], in_=o_sb[:, h * DV : (h + 1) * DV], func=ACT.Square, accum_out=ss[:, h : h + 1])
            ms = small.tile([P, HEADS], F32, tag="ms", name="ms")
            nc.gpsimd.tensor_scalar(out=ms[:], in0=ss[:], scalar1=1.0 / DV, scalar2=EPS, op0=MULT, op1=ADD)
            rinv = small.tile([P, HEADS], F32, tag="rinv", name="rinv")
            nc.gpsimd.tensor_tensor(out=rinv[:], in0=ms[:], in1=neg_half[:], op=POW)
            return rinv

        def normalize(o_sb, rinv):
            tiles = []
            for h in range(HEADS):
                t = norm.tile([P, DV], F32, tag="o_n", name="o_n")
                nc.gpsimd.tensor_scalar(
                    out=t[:].rearrange("p (t m) -> p t m", t=PACK),
                    in0=o_sb[:, h * DV : (h + 1) * DV].rearrange("p (m t) -> p t m", t=PACK),
                    scalar1=rinv[:, h : h + 1],
                    scalar2=1.0,
                    op0=MULT,
                    op1=MULT,
                )
                tiles.append(t)
            return tiles

        def turn_o(tiles):
            banks = []
            for h in range(HEADS):
                bank = ps_turn.tile([P, PACK, P], F32, tag="turn", name="o_turned")
                for t in range(PACK):
                    nc.tensor.transpose(bank[:, t, :], tiles[h][:, t * P : (t + 1) * P], ident[:])
                banks.append(bank)
            return banks

        def modulate(i, banks):
            h_grouped = group_tile("h_grouped")
            s = (i * P) // HALF
            toks = slice(i * P - s * HALF, (i + 1) * P - s * HALF)
            view = h_grouped[:].rearrange("p (g n t) -> p g n t", g=HEADS, t=PACK)
            for h in range(HEADS):
                nc.vector.tensor_tensor(
                    out=view[:, h],
                    in0=banks[h][:].rearrange("p t n -> p n t"),
                    in1=gated[h][s][:, :, toks].rearrange("p t n -> p n t"),
                    op=MULT,
                )
            return h_grouped

        def quantize_h(h_grouped):
            codes = hq.tile([P, H_PASSES * P], U32, tag="h_codes", name="h_codes", align_bytes=64)
            scales = hq.tile([P, H_PASSES * P], U8, tag="h_scales", name="h_scales", align_bytes=64)
            quantize(h_grouped, codes[:], scales[:])
            return codes, scales

        def project(i, n):
            h_codes, h_scales = codes[i]
            bank = ps_out.tile([P, HALF], F32, tag="acc", name="acc")
            cols = slice(n * HALF, (n + 1) * HALF)
            for g in range(H_PASSES):
                rows = slice(g * P, (g + 1) * P)
                nc.tensor.matmul_mx(
                    out=bank[:],
                    lhsT=h_codes[:, rows].bitcast(FP8X4),
                    lhsT_scale=h_scales[:, rows],
                    rhs=wo_codes[:, g, cols].bitcast(FP8X4),
                    rhs_scale=wo_scales[:, g, cols],
                    start=(g == 0),
                    stop=(g == H_PASSES - 1),
                )
            return bank

        def finish(i, n, bank, on_vector):
            o_tile = res.tile([P, HALF], F32, tag="o_tile", name="o_tile")
            if on_vector:
                nc.vector.tensor_copy(out=o_tile[:], in_=bank[:])
            else:
                nc.scalar.copy(out=o_tile[:], in_=bank[:])
            nc.sync.dma_start(out=out_rows[i, :, n * HALF : (n + 1) * HALF], in_=o_tile[:])

        wg_raw, x_raw, o_sb, wo_raw = {}, {}, {}, {}
        wg_raw[0, 0] = load_wg(0, 0)
        x_raw[0] = load_x(0)
        wg_raw[0, 1] = load_wg(0, 1)
        x_raw[1] = load_x(1)
        o_sb[0] = load_o(0)
        wg_raw[1, 0] = load_wg(1, 0)
        nc.sync.dma_start(out=gn_raw[:], in_=gn_weight.rearrange("(p t) -> p t", t=PACK))
        wg_raw[1, 1] = load_wg(1, 1)
        x_raw[2] = load_x(2)
        nc.gpsimd.memset(warm[:], 0.0)
        make_identity(nc, ident[:])
        nc.gpsimd.memset(neg_half[:], -0.5)
        nc.scalar.activation(out=warm[:], in_=warm[:], func=ACT.Square)

        rinv, o_n, codes = {}, {}, {}
        wide, grouped = {}, {}

        def normalize_tile(i):
            rinv[i] = stats(o_sb[i])
            o_n[i] = normalize(o_sb[i], rinv[i])

        def widen_unit(g, n, on_scalar):
            wide[g, n] = widen(wo_raw[g], g, n, on_scalar)

        x_grouped = [[group_tile(f"x_grouped_{g}") for g in range(X_PASSES)]]
        wg0 = [interleave_wg(wg_raw[0, 0])]
        turn_x(x_raw[0], 0, x_grouped[0])
        wg0.append(interleave_wg(wg_raw[0, 1]))
        turn_x(x_raw[1], 1, x_grouped[0])
        x_raw[3] = load_x(3)
        for g in range(X_PASSES):
            wg_raw[2, g] = load_wg(2, g)
        nc.sync.dma_start(out=wo_k_scale[:], in_=Wo_scale.rearrange("(g p t) o -> p g (t o)", p=P, t=PACK))
        for g in range(X_PASSES):
            quantize_wg(wg0[g], 0, g)
        quantize_x(x_grouped[0], 0)
        normalize_tile(0)
        nc.scalar.copy(out=gn[:], in_=gn_raw[:])
        gate(0, 0)

        x_grouped.append([group_tile(f"x_grouped_{g}") for g in range(X_PASSES)])
        turn_x(x_raw[2], 2, x_grouped[1])
        turn_x(x_raw[3], 3, x_grouped[1])
        prepare_wg(1, [wg_raw[1, g] for g in range(X_PASSES)])
        for g in range(X_PASSES):
            wg_raw[3, g] = load_wg(3, g)
        for g in range(H_PASSES):
            wo_raw[g] = load_wo(g)
        o_sb[1] = load_o(1)
        gate(1, 0)
        prepare_wg(2, [wg_raw[2, g] for g in range(X_PASSES)])
        o_sb[2] = load_o(2)
        quantize_x(x_grouped[1], 1)
        gate(2, 0)
        gate(0, 1)
        prepare_wg(3, [wg_raw[3, g] for g in range(X_PASSES)])
        o_sb[3] = load_o(3)
        gate(3, 0)
        gates_left = [(1, 1), (2, 1), (3, 1)]
        for g in range(H_PASSES):
            widen_unit(g, 0, SW_A[g])
            if g >= 1:
                grouped[g - 1, 0] = interleave_wo(wide[g - 1, 0])
            if g >= 2:
                quantize_wo(grouped[g - 2, 0], g - 2, 0)
            if g < GATES_EARLY:
                gate(*gates_left.pop(0))
        grouped[3, 0] = interleave_wo(wide[3, 0])
        quantize_wo(grouped[2, 0], 2, 0)
        turned = {0: turn_o(o_n[0])}
        normalize_tile(1)
        quantize_wo(grouped[3, 0], 3, 0)

        ready, backlog = [], []
        second_done = 0

        def drain(count, on_vector):
            for k in range(count):
                if ready:
                    j, n, b = ready.pop(0)
                    finish(j, n, b, on_vector)

        for i in range(TILES):
            h_grouped = modulate(i, turned[i])
            if i + 4 < TILES:
                o_sb[i + 4] = load_o(i + 4)
            for g in WIDEN_B.get(i, ()):
                widen_unit(g, 1, SW_B)
            if gates_left and i >= GATE_STEP:
                gate(*gates_left.pop(0))
            if i + 2 < TILES:
                normalize_tile(i + 2)
            for g in B_INT.get(i, ()):
                grouped[g, 1] = interleave_wo(wide[g, 1], g in B_G)
            drain(1, OUTV[i])
            if i + 1 < TILES:
                turned[i + 1] = turn_o(o_n[i + 1])
            codes[i] = quantize_h(h_grouped)
            for g in B_Q.get(i, ()):
                quantize_wo(grouped[g, 1], g, 1)
                second_done += 1
            backlog.append(i)
            drain(1, OUTV[i])
            ready.append((i, 0, project(i, 0)))
            if second_done == H_PASSES:
                for k in range(MAXB[i]):
                    if backlog:
                        j = backlog.pop(0)
                        if len(ready) == 2:
                            drain(1, k % 2 == 1)
                        ready.append((j, 1, project(j, 1)))
        k = 0
        while backlog:
            drain(1, k % 2 == 0)
            k += 1
            j = backlog.pop(0)
            ready.append((j, 1, project(j, 1)))
        while ready:
            drain(1, k % 2 == 0)
            k += 1
